import numpy as np
import ml_dtypes


def mxq(x, axis, fmt="e4m3"):
    dtype, down = {"e4m3": (ml_dtypes.float8_e4m3fn, 7), "e5m2": (ml_dtypes.float8_e5m2, 14)}[fmt]
    v = np.moveaxis(np.asarray(x, np.float32).astype(ml_dtypes.bfloat16).astype(np.float64), axis, -1)
    blocks = v.reshape(v.shape[:-1] + (-1, 32))
    amax = np.abs(blocks).max(-1, keepdims=True)
    byte = np.maximum(np.where(amax > 0, np.frexp(amax)[1] - 1 + 127, 0) - down, 1)
    scale = np.exp2(byte - 127.0)
    codes = (blocks / scale).astype(np.float32).astype(dtype).astype(np.float64)
    return np.moveaxis((codes * scale).reshape(v.shape), -1, axis)


WIDE = False


def mx_kscale(k):
    if not WIDE:
        return np.ones(k)
    levels = np.array([10, -10, 5, -5, 0])
    a = np.random.permutation(np.resize(levels, k // 512 * 4)).reshape(k // 512, 4)
    idx = np.arange(k)
    return np.exp2(a[idx // 512, idx % 128 // 32])


BF16 = ml_dtypes.bfloat16


def bf(x):
    return np.asarray(x, np.float32).astype(BF16)


def f64(x):
    return np.asarray(x).astype(np.float64)


B, N_EP, S, D, IN_DIM, L, K = 6, 3, 512, 256, 255, 512, 10


def setup_inputs():
    s, t = mx_kscale(S), mx_kscale(L)
    r = np.random.standard_normal
    g = r((B, S, S)) * 1.56
    a = np.exp(g - g.max(-1, keepdims=True))
    a = a / a.sum(-1, keepdims=True)
    return {"attn1": bf(a * s), "v1": bf(r((B, S, L)) * 4.0 / s[:, None] * t),
            "Wq2": bf(r((L, L)) * 4.0 / np.sqrt(L) / t[:, None]), "bq2": bf(r(L) * 0.2),
            "Wk2": bf(r((L, L)) * 4.0 / np.sqrt(L) / t[:, None]), "bk2": bf(r(L) * 0.2),
            "Wv2": bf(r((L, L)) * 3.2 / np.sqrt(L) / t[:, None]), "bv2": bf(r(L) * 0.2)}


def reference(attn1, v1, Wq2, bq2, Wk2, bk2, Wv2, bv2):
    h = np.maximum(mxq(f64(attn1), 2, "e4m3") @ mxq(f64(v1), 1, "e4m3"), 0.0)
    hq = mxq(h, 2, "e4m3")
    q2 = (hq @ mxq(f64(Wq2), 0, "e4m3")) + f64(bq2)
    k2 = (hq @ mxq(f64(Wk2), 0, "e4m3")) + f64(bk2)
    v2 = (hq @ mxq(f64(Wv2), 0, "e4m3")) + f64(bv2)
    return q2, k2, v2

@@ -1,0 +1,221 @@
+from contextlib import ExitStack
+
+import concourse.mybir as mybir
+from concourse.masks import make_identity
+
+BF16 = mybir.dt.bfloat16
+F32 = mybir.dt.float32
+U32 = mybir.dt.uint32
+U8 = mybir.dt.uint8
+FP8X4 = mybir.dt.float8_e4m3fn_x4
+RELU = mybir.ActivationFunctionType.Relu
+ADD = mybir.AluOpType.add
+
+P = 128
+PACK = 4
+SETS = 6
+SIZE = P * PACK
+TILES = SIZE // P
+OUTPUTS = 3
+RUN = 4
+STAGED = 6
+
+FLOPS = 2 * SETS * SIZE * SIZE * SIZE * (1 + OUTPUTS)
+
+
+def tile_perspectronencodernetwork_pa_kernel(
+    tc, attn1, v1, Wq2, bq2, Wk2, bk2, Wv2, bv2, out_0, out_1, out_2
+):
+    nc = tc.nc
+    weights = (Wq2, Wk2, Wv2)
+    biases = (bq2, bk2, bv2)
+    outs = (out_0, out_1, out_2)
+
+    with ExitStack() as ctx:
+        const = ctx.enter_context(tc.tile_pool(name="const", bufs=1))
+        resident = ctx.enter_context(tc.tile_pool(name="resident", bufs=1))
+        work = ctx.enter_context(tc.tile_pool(name="work", bufs=2))
+        staging = ctx.enter_context(tc.tile_pool(name="staging", bufs=STAGED))
+        psum_flip = ctx.enter_context(tc.psum_pool(name="psum_flip", bufs=2))
+        psum_hidden = ctx.enter_context(tc.psum_pool(name="psum_hidden", bufs=2))
+        psum_out = ctx.enter_context(tc.psum_pool(name="psum_out", bufs=4))
+
+        bias_rows = const.tile([P, OUTPUTS * SIZE], BF16, name="bias_rows")
+        nc.vector.memset(bias_rows[:], 0.0)
+        ones = const.tile([P, P], BF16, name="ones")
+        nc.vector.memset(ones[:], 1.0)
+        identity = const.tile([P, P], F32, name="identity")
+        make_identity(nc, identity[:])
+        table_warm = const.tile([P, 1], F32, name="table_warm")
+        nc.scalar.activation(out=table_warm[:], in_=ones[:, 0:1], func=RELU)
+
+        attn_sb = [resident.tile([P, PACK * SIZE], BF16, name="attn_sb%d" % b) for b in range(SETS)]
+        val_sb = [resident.tile([P, PACK * SIZE], BF16, name="val_sb%d" % b) for b in range(SETS)]
+        w_sb = [resident.tile([P, PACK * SIZE], BF16, name="w_sb%d" % x) for x in range(OUTPUTS)]
+
+        def load_set(b):
+            nc.sync.dma_start(
+                out=attn_sb[b][:], in_=attn1[b].rearrange("(p j) k -> p (j k)", j=TILES)
+            )
+            nc.sync.dma_start(
+                out=val_sb[b][:].rearrange("p (u r) -> p u r", u=2),
+                in_=v1[b].rearrange("(u p e) f -> p u (e f)", u=2, e=2),
+            )
+
+        load_set(0)
+        for x in range(OUTPUTS):
+            nc.sync.dma_start(
+                out=bias_rows[0:1, x * SIZE : (x + 1) * SIZE],
+                in_=biases[x].rearrange("(o n) -> o n", o=1),
+            )
+        for x in range(OUTPUTS):
+            nc.sync.dma_start(
+                out=w_sb[x][:].rearrange("p (t o) -> p t o", t=PACK),
+                in_=weights[x].rearrange("(t p) o -> p t o", t=PACK),
+            )
+        for b in range(1, SETS):
+            load_set(b)
+
+        attn_grouped, attn_mx = {}, {}
+        val_grouped, val_mx = {}, {}
+        hidden_mx = {}
+        w_mx = {}
+
+        def regroup(copy, grouped, rows):
+            copy(
+                out=grouped[:].rearrange("p (c i t) -> p c t i", i=RUN, t=PACK),
+                in_=rows[:].rearrange("p (t c i) -> p c t i", t=PACK, i=RUN),
+            )
+
+        def quantise(name, grouped, bufs):
+            columns = grouped.shape[1] // PACK
+            words = work.tile([P, columns], U32, name=name + "_words", bufs=bufs, align_bytes=64)
+            scales = work.tile([P, columns], U8, name=name + "_scales", bufs=bufs, align_bytes=64)
+            nc.vector.quantize_mx(out=words[:].bitcast(FP8X4), scales=scales[:], in_=grouped)
+            return words, scales
+
+        def multiply(out, stationary, stationary_cols, moving, moving_cols):
+            nc.tensor.matmul_mx(
+                out=out,
+                lhsT=stationary[0][:, stationary_cols].bitcast(FP8X4),
+                lhsT_scale=stationary[1][:, stationary_cols],
+                rhs=moving[0][:, moving_cols].bitcast(FP8X4),
+                rhs_scale=moving[1][:, moving_cols],
+                start=True,
+                stop=True,
+            )
+
+        def tile_cols(i):
+            return slice(i * P, (i + 1) * P)
+
+        def transpose_attention(b):
+            words = attn_sb[b][:].bitcast(F32)
+            grouped = work.tile([P, PACK * SIZE], BF16, name="attn_grouped", align_bytes=64)
+            grouped_words = grouped[:].bitcast(F32).rearrange(
+                "p (j q u) -> p j q u", j=TILES, u=2
+            )
+            for pair in range(TILES // 2):
+                flipped = psum_flip.tile([P, 2, 2, P], F32, name="flipped")
+                for i in range(2):
+                    for u in range(2):
+                        nc.tensor.transpose(
+                            flipped[:, i, u, :],
+                            words[:, tile_cols(2 * (2 * pair + i) + u)],
+                            identity[:],
+                        )
+                nc.scalar.copy(
+                    out=grouped_words[:, 2 * pair : 2 * pair + 2, :, :],
+                    in_=flipped[:].rearrange("p i u q -> p i q u"),
+                )
+            attn_grouped[b] = grouped
+
+        def quantise_attention(b):
+            attn_mx[b] = quantise("attn", attn_grouped[b][:], 2)
+
+        def regroup_values(b, copy):
+            grouped = work.tile([P, PACK * SIZE], BF16, name="val_grouped", align_bytes=64)
+            regroup(copy, grouped, val_sb[b])
+            val_grouped[b] = grouped
+
+        def quantise_values(b):
+            val_mx[b] = quantise("val", val_grouped[b][:], 2)
+
+        def prepare_weight(x, copy):
+            grouped = work.tile([P, PACK * SIZE], BF16, name="w_grouped", align_bytes=64)
+            regroup(copy, grouped, w_sb[x])
+            w_mx[x] = quantise("w%d" % x, grouped[:], 1)
+
+        bias_sb = const.tile([P, OUTPUTS, SIZE], BF16, name="bias_sb")
+
+        def spread_biases():
+            for x in range(OUTPUTS):
+                spread = psum_out.tile([P, SIZE], BF16, name="spread", tag="projected")
+                nc.tensor.matmul(
+                    spread[:],
+                    lhsT=ones[:],
+                    rhs=bias_rows[:, x * SIZE : (x + 1) * SIZE],
+                    start=True,
+                    stop=True,
+                )
+                nc.vector.tensor_copy(out=bias_sb[:, x, :], in_=spread[:])
+
+        def hidden(b, j):
+            product = psum_hidden.tile([P, PACK, P], F32, name="product")
+            for t in range(PACK):
+                multiply(product[:, t, :], val_mx[b], tile_cols(t), attn_mx[b], tile_cols(j))
+            grouped = work.tile([P, P, PACK], BF16, name="hidden_grouped", align_bytes=64)
+            nc.scalar.activation(
+                out=grouped[:], in_=product[:].rearrange("p t q -> p q t"), func=RELU
+            )
+            hidden_mx[(b, j)] = quantise(
+                "hidden", grouped[:].rearrange("p q t -> p (q t)"), 2 * TILES
+            )
+
+        def project(b, x):
+            last = b == SETS - 1 and x == OUTPUTS - 1
+            tiles_per_store = 1 if last else TILES
+            out_rows = outs[x][b].rearrange("(p j) o -> p j o", j=TILES)
+            staged = staging.tile([P, TILES, SIZE], F32, name="staged")
+            for j in range(TILES):
+                projected = psum_out.tile([P, SIZE], F32, name="projected")
+                multiply(projected[:], hidden_mx[(b, j)], slice(0, P), w_mx[x], slice(0, SIZE))
+                nc.vector.tensor_tensor(
+                    out=staged[:, j, :], in0=projected[:], in1=bias_sb[:, x, :], op=ADD
+                )
+                if (j + 1) % tiles_per_store == 0:
+                    done = slice(j + 1 - tiles_per_store, j + 1)
+                    nc.sync.dma_start(out=out_rows[:, done, :], in_=staged[:, done, :])
+
+        transpose_attention(0)
+        regroup_values(0, nc.vector.tensor_copy)
+        quantise_attention(0)
+        quantise_values(0)
+        prepare_weight(0, nc.scalar.copy)
+        prepare_weight(1, nc.vector.tensor_copy)
+        spread_biases()
+        for j in range(TILES):
+            hidden(0, j)
+        prepare_weight(2, nc.scalar.copy)
+        transpose_attention(1)
+        regroup_values(1, nc.scalar.copy)
+        quantise_attention(1)
+        quantise_values(1)
+
+        for b in range(SETS):
+            project(b, 0)
+            if b + 1 < SETS:
+                hidden(b + 1, 0)
+                hidden(b + 1, 1)
+            if b + 2 < SETS:
+                transpose_attention(b + 2)
+            project(b, 1)
+            if b + 2 < SETS:
+                quantise_attention(b + 2)
+            if b + 1 < SETS:
+                hidden(b + 1, 2)
+                hidden(b + 1, 3)
+            if b + 2 < SETS:
+                regroup_values(b + 2, nc.scalar.copy)
+            project(b, 2)
+            if b + 2 < SETS:
+                quantise_values(b + 2)

@@ -179,9 +179,15 @@ def tile_perspectronencodernetwork_pa_kernel(
             for j in range(TILES):
                 projected = psum_out.tile([P, SIZE], F32, name="projected")
                 multiply(projected[:], hidden_mx[(b, j)], slice(0, P), w_mx[x], slice(0, SIZE))
-                nc.vector.tensor_tensor(
-                    out=staged[:, j, :], in0=projected[:], in1=bias_sb[:, x, :], op=ADD
-                )
+                if j == 0:
+                    nc.scalar.copy(out=staged[:, j, :], in_=projected[:])
+                    nc.gpsimd.tensor_tensor(
+                        out=staged[:, j, :], in0=staged[:, j, :], in1=bias_sb[:, x, :], op=ADD
+                    )
+                else:
+                    nc.vector.tensor_tensor(
+                        out=staged[:, j, :], in0=projected[:], in1=bias_sb[:, x, :], op=ADD
+                    )
                 if (j + 1) % tiles_per_store == 0:
                     done = slice(j + 1 - tiles_per_store, j + 1)
                     nc.sync.dma_start(out=out_rows[:, done, :], in_=staged[:, done, :])

@@ -39,6 +39,7 @@ def tile_perspectronencodernetwork_pa_kernel(
         psum_flip = ctx.enter_context(tc.psum_pool(name="psum_flip", bufs=2))
         psum_hidden = ctx.enter_context(tc.psum_pool(name="psum_hidden", bufs=2))
         psum_out = ctx.enter_context(tc.psum_pool(name="psum_out", bufs=4))
+        ctx.enter_context(tc.manual_schedule())
 
         bias_rows = const.tile([P, OUTPUTS * SIZE], BF16, name="bias_rows")
         nc.vector.memset(bias_rows[:], 0.0)
@@ -63,6 +64,7 @@ def tile_perspectronencodernetwork_pa_kernel(
             )
 
         load_set(0)
+        load_set(1)
         for x in range(OUTPUTS):
             nc.sync.dma_start(
                 out=bias_rows[0:1, x * SIZE : (x + 1) * SIZE],
@@ -73,13 +75,14 @@ def tile_perspectronencodernetwork_pa_kernel(
                 out=w_sb[x][:].rearrange("p (t o) -> p t o", t=PACK),
                 in_=weights[x].rearrange("(t p) o -> p t o", t=PACK),
             )
-        for b in range(1, SETS):
+        for b in range(2, SETS):
             load_set(b)
 
         attn_grouped, attn_mx = {}, {}
         val_grouped, val_mx = {}, {}
-        hidden_mx = {}
+        hidden_grouped, hidden_mx = {}, {}
         w_mx = {}
+        staged = {}
 
         def regroup(copy, grouped, rows):
             copy(
@@ -159,69 +162,72 @@ def tile_perspectronencodernetwork_pa_kernel(
                 )
                 nc.vector.tensor_copy(out=bias_sb[:, x, :], in_=spread[:])
 
-        def hidden(b, j):
+        def hidden_product(b, j):
+            if j == 0:
+                hidden_grouped[b] = work.tile(
+                    [P, TILES, P, PACK], BF16, name="hidden_grouped", align_bytes=64
+                )
             product = psum_hidden.tile([P, PACK, P], F32, name="product")
             for t in range(PACK):
                 multiply(product[:, t, :], val_mx[b], tile_cols(t), attn_mx[b], tile_cols(j))
-            grouped = work.tile([P, P, PACK], BF16, name="hidden_grouped", align_bytes=64)
             nc.scalar.activation(
-                out=grouped[:], in_=product[:].rearrange("p t q -> p q t"), func=RELU
-            )
-            hidden_mx[(b, j)] = quantise(
-                "hidden", grouped[:].rearrange("p q t -> p (q t)"), 2 * TILES
+                out=hidden_grouped[b][:, j, :, :],
+                in_=product[:].rearrange("p t q -> p q t"),
+                func=RELU,
             )
 
-        def project(b, x):
+        def quantise_hidden(b):
+            hidden_mx[b] = quantise(
+                "hidden", hidden_grouped[b][:].rearrange("p j q t -> p (j q t)"), 2
+            )
+
+        def project_tile(b, x, j):
+            if j == 0:
+                staged[(b, x)] = staging.tile([P, TILES, SIZE], F32, name="staged")
+            rows = staged[(b, x)]
+            projected = psum_out.tile([P, SIZE], F32, name="projected")
+            multiply(projected[:], hidden_mx[b], tile_cols(j), w_mx[x], slice(0, SIZE))
+            if j == 0:
+                nc.scalar.copy(out=rows[:, j, :], in_=projected[:])
+                nc.gpsimd.tensor_tensor(
+                    out=rows[:, j, :], in0=rows[:, j, :], in1=bias_sb[:, x, :], op=ADD
+                )
+            else:
+                nc.vector.tensor_tensor(
+                    out=rows[:, j, :], in0=projected[:], in1=bias_sb[:, x, :], op=ADD
+                )
             last = b == SETS - 1 and x == OUTPUTS - 1
             tiles_per_store = 1 if last else TILES
-            out_rows = outs[x][b].rearrange("(p j) o -> p j o", j=TILES)
-            staged = staging.tile([P, TILES, SIZE], F32, name="staged")
-            for j in range(TILES):
-                projected = psum_out.tile([P, SIZE], F32, name="projected")
-                multiply(projected[:], hidden_mx[(b, j)], slice(0, P), w_mx[x], slice(0, SIZE))
-                if j == 0:
-                    nc.scalar.copy(out=staged[:, j, :], in_=projected[:])
-                    nc.gpsimd.tensor_tensor(
-                        out=staged[:, j, :], in0=staged[:, j, :], in1=bias_sb[:, x, :], op=ADD
-                    )
-                else:
-                    nc.vector.tensor_tensor(
-                        out=staged[:, j, :], in0=projected[:], in1=bias_sb[:, x, :], op=ADD
-                    )
-                if (j + 1) % tiles_per_store == 0:
-                    done = slice(j + 1 - tiles_per_store, j + 1)
-                    nc.sync.dma_start(out=out_rows[:, done, :], in_=staged[:, done, :])
+            if (j + 1) % tiles_per_store == 0:
+                done = slice(j + 1 - tiles_per_store, j + 1)
+                out_rows = outs[x][b].rearrange("(p j) o -> p j o", j=TILES)
+                nc.sync.dma_start(out=out_rows[:, done, :], in_=rows[:, done, :])
 
-        transpose_attention(0)
-        regroup_values(0, nc.vector.tensor_copy)
-        quantise_attention(0)
-        quantise_values(0)
-        prepare_weight(0, nc.scalar.copy)
+        def prepare(b):
+            transpose_attention(b)
+            regroup_values(b, nc.vector.tensor_copy if b < 2 else nc.scalar.copy)
+
+        def quantise_inputs(b):
+            quantise_attention(b)
+            quantise_values(b)
+
+        prepare(0)
+        quantise_inputs(0)
+        prepare(1)
+        for j in range(TILES):
+            hidden_product(0, j)
+        prepare_weight(0, nc.vector.tensor_copy)
         prepare_weight(1, nc.vector.tensor_copy)
         spread_biases()
-        for j in range(TILES):
-            hidden(0, j)
         prepare_weight(2, nc.scalar.copy)
-        transpose_attention(1)
-        regroup_values(1, nc.scalar.copy)
-        quantise_attention(1)
-        quantise_values(1)
 
         for b in range(SETS):
-            project(b, 0)
+            quantise_hidden(b)
             if b + 1 < SETS:
-                hidden(b + 1, 0)
-                hidden(b + 1, 1)
+                quantise_inputs(b + 1)
             if b + 2 < SETS:
-                transpose_attention(b + 2)
-            project(b, 1)
-            if b + 2 < SETS:
-                quantise_attention(b + 2)
-            if b + 1 < SETS:
-                hidden(b + 1, 2)
-                hidden(b + 1, 3)
-            if b + 2 < SETS:
-                regroup_values(b + 2, nc.scalar.copy)
-            project(b, 2)
-            if b + 2 < SETS:
-                quantise_values(b + 2)
+                prepare(b + 2)
+            for step in range(OUTPUTS * TILES):
+                project_tile(b, step // TILES, step % TILES)
+                if b + 1 < SETS and step % OUTPUTS == OUTPUTS - 1:
+                    hidden_product(b + 1, step // OUTPUTS)

@@ -18,7 +18,8 @@ SIZE = P * PACK
 TILES = SIZE // P
 OUTPUTS = 3
 RUN = 4
-STAGED = 6
+STAGED = 8
+GPSIMD_TILE = (0, 2, 0)
 
 FLOPS = 2 * SETS * SIZE * SIZE * SIZE * (1 + OUTPUTS)
 
@@ -34,7 +35,7 @@ def tile_perspectronencodernetwork_pa_kernel(
     with ExitStack() as ctx:
         const = ctx.enter_context(tc.tile_pool(name="const", bufs=1))
         resident = ctx.enter_context(tc.tile_pool(name="resident", bufs=1))
-        work = ctx.enter_context(tc.tile_pool(name="work", bufs=2))
+        work = ctx.enter_context(tc.tile_pool(name="work", bufs=3))
         staging = ctx.enter_context(tc.tile_pool(name="staging", bufs=STAGED))
         psum_flip = ctx.enter_context(tc.psum_pool(name="psum_flip", bufs=2))
         psum_hidden = ctx.enter_context(tc.psum_pool(name="psum_hidden", bufs=2))
@@ -54,40 +55,50 @@ def tile_perspectronencodernetwork_pa_kernel(
         val_sb = [resident.tile([P, PACK * SIZE], BF16, name="val_sb%d" % b) for b in range(SETS)]
         w_sb = [resident.tile([P, PACK * SIZE], BF16, name="w_sb%d" % x) for x in range(OUTPUTS)]
 
-        def load_set(b):
+        def load_attention(b):
             nc.sync.dma_start(
                 out=attn_sb[b][:], in_=attn1[b].rearrange("(p j) k -> p (j k)", j=TILES)
             )
+
+        def load_values(b):
             nc.sync.dma_start(
                 out=val_sb[b][:].rearrange("p (u r) -> p u r", u=2),
                 in_=v1[b].rearrange("(u p e) f -> p u (e f)", u=2, e=2),
             )
 
-        load_set(0)
-        load_set(1)
+        def load_weight(x):
+            nc.sync.dma_start(
+                out=w_sb[x][:].rearrange("p (t o) -> p t o", t=PACK),
+                in_=weights[x].rearrange("(t p) o -> p t o", t=PACK),
+            )
+
+        load_weight(0)
         for x in range(OUTPUTS):
             nc.sync.dma_start(
                 out=bias_rows[0:1, x * SIZE : (x + 1) * SIZE],
                 in_=biases[x].rearrange("(o n) -> o n", o=1),
             )
-        for x in range(OUTPUTS):
-            nc.sync.dma_start(
-                out=w_sb[x][:].rearrange("p (t o) -> p t o", t=PACK),
-                in_=weights[x].rearrange("(t p) o -> p t o", t=PACK),
-            )
-        for b in range(2, SETS):
-            load_set(b)
+        load_attention(0)
+        load_values(0)
+        load_weight(1)
+        load_weight(2)
+        for b in range(1, SETS):
+            load_values(b)
+            load_attention(b)
 
         attn_grouped, attn_mx = {}, {}
         val_grouped, val_mx = {}, {}
         hidden_grouped, hidden_mx = {}, {}
-        w_mx = {}
+        w_grouped, w_mx = {}, {}
+        flips = {}
         staged = {}
 
-        def regroup(copy, grouped, rows):
+        def regroup(copy, grouped, rows, half):
+            runs = SIZE // RUN // 2
+            some = slice(half * runs, (half + 1) * runs)
             copy(
-                out=grouped[:].rearrange("p (c i t) -> p c t i", i=RUN, t=PACK),
-                in_=rows[:].rearrange("p (t c i) -> p c t i", t=PACK, i=RUN),
+                out=grouped[:].rearrange("p (c i t) -> p c t i", i=RUN, t=PACK)[:, some],
+                in_=rows[:].rearrange("p (t c i) -> p c t i", t=PACK, i=RUN)[:, some],
             )
 
         def quantise(name, grouped, bufs):
@@ -113,10 +124,6 @@ def tile_perspectronencodernetwork_pa_kernel(
 
         def transpose_attention(b):
             words = attn_sb[b][:].bitcast(F32)
-            grouped = work.tile([P, PACK * SIZE], BF16, name="attn_grouped", align_bytes=64)
-            grouped_words = grouped[:].bitcast(F32).rearrange(
-                "p (j q u) -> p j q u", j=TILES, u=2
-            )
             for pair in range(TILES // 2):
                 flipped = psum_flip.tile([P, 2, 2, P], F32, name="flipped")
                 for i in range(2):
@@ -126,27 +133,41 @@ def tile_perspectronencodernetwork_pa_kernel(
                             words[:, tile_cols(2 * (2 * pair + i) + u)],
                             identity[:],
                         )
-                nc.scalar.copy(
-                    out=grouped_words[:, 2 * pair : 2 * pair + 2, :, :],
-                    in_=flipped[:].rearrange("p i u q -> p i q u"),
+                flips[(b, pair)] = flipped
+
+        def group_attention(b, pair):
+            if pair == 0:
+                attn_grouped[b] = work.tile(
+                    [P, PACK * SIZE], BF16, name="attn_grouped", align_bytes=64
                 )
-            attn_grouped[b] = grouped
+            grouped_words = attn_grouped[b][:].bitcast(F32).rearrange(
+                "p (j q u) -> p j q u", j=TILES, u=2
+            )
+            nc.scalar.copy(
+                out=grouped_words[:, 2 * pair : 2 * pair + 2, :, :],
+                in_=flips[(b, pair)][:].rearrange("p i u q -> p i q u"),
+            )
 
         def quantise_attention(b):
-            attn_mx[b] = quantise("attn", attn_grouped[b][:], 2)
+            attn_mx[b] = quantise("attn", attn_grouped[b][:], 3)
 
-        def regroup_values(b, copy):
-            grouped = work.tile([P, PACK * SIZE], BF16, name="val_grouped", align_bytes=64)
-            regroup(copy, grouped, val_sb[b])
-            val_grouped[b] = grouped
+        def regroup_values(b, half, copy):
+            if half == 0:
+                val_grouped[b] = work.tile(
+                    [P, PACK * SIZE], BF16, name="val_grouped", align_bytes=64
+                )
+            regroup(copy, val_grouped[b], val_sb[b], half)
 
         def quantise_values(b):
-            val_mx[b] = quantise("val", val_grouped[b][:], 2)
+            val_mx[b] = quantise("val", val_grouped[b][:], 3)
 
-        def prepare_weight(x, copy):
-            grouped = work.tile([P, PACK * SIZE], BF16, name="w_grouped", align_bytes=64)
-            regroup(copy, grouped, w_sb[x])
-            w_mx[x] = quantise("w%d" % x, grouped[:], 1)
+        def regroup_weight(x, copy):
+            w_grouped[x] = work.tile([P, PACK * SIZE], BF16, name="w_grouped", align_bytes=64)
+            for half in range(2):
+                regroup(copy, w_grouped[x], w_sb[x], half)
+
+        def quantise_weight(x):
+            w_mx[x] = quantise("w%d" % x, w_grouped[x][:], 1)
 
         bias_sb = const.tile([P, OUTPUTS, SIZE], BF16, name="bias_sb")
 
@@ -160,9 +181,9 @@ def tile_perspectronencodernetwork_pa_kernel(
                     start=True,
                     stop=True,
                 )
-                nc.vector.tensor_copy(out=bias_sb[:, x, :], in_=spread[:])
+                nc.scalar.copy(out=bias_sb[:, x, :], in_=spread[:])
 
-        def hidden_product(b, j):
+        def hidden_product(b, j, relu=None):
             if j == 0:
                 hidden_grouped[b] = work.tile(
                     [P, TILES, P, PACK], BF16, name="hidden_grouped", align_bytes=64
@@ -170,15 +191,16 @@ def tile_perspectronencodernetwork_pa_kernel(
             product = psum_hidden.tile([P, PACK, P], F32, name="product")
             for t in range(PACK):
                 multiply(product[:, t, :], val_mx[b], tile_cols(t), attn_mx[b], tile_cols(j))
-            nc.scalar.activation(
-                out=hidden_grouped[b][:, j, :, :],
-                in_=product[:].rearrange("p t q -> p q t"),
-                func=RELU,
-            )
+            hidden = hidden_grouped[b][:, j, :, :]
+            read = product[:].rearrange("p t q -> p q t")
+            if relu == "vector":
+                nc.vector.tensor_scalar_max(hidden, read, 0.0)
+            else:
+                nc.scalar.activation(out=hidden, in_=read, func=RELU)
 
         def quantise_hidden(b):
             hidden_mx[b] = quantise(
-                "hidden", hidden_grouped[b][:].rearrange("p j q t -> p (j q t)"), 2
+                "hidden", hidden_grouped[b][:].rearrange("p j q t -> p (j q t)"), 3
             )
 
         def project_tile(b, x, j):
@@ -187,7 +209,7 @@ def tile_perspectronencodernetwork_pa_kernel(
             rows = staged[(b, x)]
             projected = psum_out.tile([P, SIZE], F32, name="projected")
             multiply(projected[:], hidden_mx[b], tile_cols(j), w_mx[x], slice(0, SIZE))
-            if j == 0:
+            if j == GPSIMD_TILE[x]:
                 nc.scalar.copy(out=rows[:, j, :], in_=projected[:])
                 nc.gpsimd.tensor_tensor(
                     out=rows[:, j, :], in0=rows[:, j, :], in1=bias_sb[:, x, :], op=ADD
@@ -203,31 +225,50 @@ def tile_perspectronencodernetwork_pa_kernel(
                 out_rows = outs[x][b].rearrange("(p j) o -> p j o", j=TILES)
                 nc.sync.dma_start(out=out_rows[:, done, :], in_=rows[:, done, :])
 
-        def prepare(b):
-            transpose_attention(b)
-            regroup_values(b, nc.vector.tensor_copy if b < 2 else nc.scalar.copy)
-
-        def quantise_inputs(b):
-            quantise_attention(b)
-            quantise_values(b)
-
-        prepare(0)
-        quantise_inputs(0)
-        prepare(1)
-        for j in range(TILES):
-            hidden_product(0, j)
-        prepare_weight(0, nc.vector.tensor_copy)
-        prepare_weight(1, nc.vector.tensor_copy)
+        vector_copy, scalar_copy = nc.vector.tensor_copy, nc.scalar.copy
         spread_biases()
-        prepare_weight(2, nc.scalar.copy)
+        regroup_weight(0, vector_copy)
+        quantise_weight(0)
+        transpose_attention(0)
+        for half in range(2):
+            regroup_values(0, half, vector_copy)
+        for pair in range(2):
+            group_attention(0, pair)
+        regroup_weight(1, scalar_copy)
+        quantise_values(0)
+        quantise_attention(0)
+        regroup_weight(2, vector_copy)
+        quantise_weight(2)
+        quantise_weight(1)
+        for j in range(TILES - 1):
+            hidden_product(0, j)
+        regroup_values(1, 0, vector_copy)
+        hidden_product(0, TILES - 1, "vector")
+        quantise_hidden(0)
+        transpose_attention(1)
+        regroup_values(1, 1, vector_copy)
+        quantise_values(1)
+        for pair in range(2):
+            group_attention(1, pair)
+        regroup_values(2, 0, scalar_copy)
+        quantise_attention(1)
 
         for b in range(SETS):
-            quantise_hidden(b)
-            if b + 1 < SETS:
-                quantise_inputs(b + 1)
-            if b + 2 < SETS:
-                prepare(b + 2)
+            near, far, next_far = b + 1, b + 2, b + 3
             for step in range(OUTPUTS * TILES):
                 project_tile(b, step // TILES, step % TILES)
-                if b + 1 < SETS and step % OUTPUTS == OUTPUTS - 1:
-                    hidden_product(b + 1, step // OUTPUTS)
+                if far < SETS and step == 1:
+                    transpose_attention(far)
+                    regroup_values(far, 1, scalar_copy)
+                if near < SETS and step in (3, 4, 6, 7):
+                    hidden_product(near, (3, 4, 6, 7).index(step))
+                if far < SETS and step == 5:
+                    quantise_values(far)
+                if far < SETS and step in (8, 9):
+                    group_attention(far, step - 8)
+                if near < SETS and step == 9:
+                    quantise_hidden(near)
+                if next_far < SETS and step == 9:
+                    regroup_values(next_far, 0, scalar_copy)
+                if far < SETS and step == 11:
+                    quantise_attention(far)

from contextlib import ExitStack

import concourse.mybir as mybir
from concourse.masks import make_identity

BF16 = mybir.dt.bfloat16
F32 = mybir.dt.float32
U32 = mybir.dt.uint32
U8 = mybir.dt.uint8
FP8X4 = mybir.dt.float8_e4m3fn_x4
RELU = mybir.ActivationFunctionType.Relu
ADD = mybir.AluOpType.add

P = 128
PACK = 4
SETS = 6
SIZE = P * PACK
TILES = SIZE // P
OUTPUTS = 3
RUN = 4
STAGED = 8
GPSIMD_TILE = (0, 2, 0)

FLOPS = 2 * SETS * SIZE * SIZE * SIZE * (1 + OUTPUTS)


def tile_perspectronencodernetwork_pa_kernel(
    tc, attn1, v1, Wq2, bq2, Wk2, bk2, Wv2, bv2, out_0, out_1, out_2
):
    nc = tc.nc
    weights = (Wq2, Wk2, Wv2)
    biases = (bq2, bk2, bv2)
    outs = (out_0, out_1, out_2)

    with ExitStack() as ctx:
        const = ctx.enter_context(tc.tile_pool(name="const", bufs=1))
        resident = ctx.enter_context(tc.tile_pool(name="resident", bufs=1))
        work = ctx.enter_context(tc.tile_pool(name="work", bufs=3))
        staging = ctx.enter_context(tc.tile_pool(name="staging", bufs=STAGED))
        psum_flip = ctx.enter_context(tc.psum_pool(name="psum_flip", bufs=2))
        psum_hidden = ctx.enter_context(tc.psum_pool(name="psum_hidden", bufs=2))
        psum_out = ctx.enter_context(tc.psum_pool(name="psum_out", bufs=4))
        ctx.enter_context(tc.manual_schedule())

        bias_rows = const.tile([P, OUTPUTS * SIZE], BF16, name="bias_rows")
        nc.vector.memset(bias_rows[:], 0.0)
        ones = const.tile([P, P], BF16, name="ones")
        nc.vector.memset(ones[:], 1.0)
        identity = const.tile([P, P], F32, name="identity")
        make_identity(nc, identity[:])
        table_warm = const.tile([P, 1], F32, name="table_warm")
        nc.scalar.activation(out=table_warm[:], in_=ones[:, 0:1], func=RELU)

        attn_sb = [resident.tile([P, PACK * SIZE], BF16, name="attn_sb%d" % b) for b in range(SETS)]
        val_sb = [resident.tile([P, PACK * SIZE], BF16, name="val_sb%d" % b) for b in range(SETS)]
        w_sb = [resident.tile([P, PACK * SIZE], BF16, name="w_sb%d" % x) for x in range(OUTPUTS)]

        def load_attention(b):
            nc.sync.dma_start(
                out=attn_sb[b][:], in_=attn1[b].rearrange("(p j) k -> p (j k)", j=TILES)
            )

        def load_values(b):
            nc.sync.dma_start(
                out=val_sb[b][:].rearrange("p (u r) -> p u r", u=2),
                in_=v1[b].rearrange("(u p e) f -> p u (e f)", u=2, e=2),
            )

        def load_weight(x):
            nc.sync.dma_start(
                out=w_sb[x][:].rearrange("p (t o) -> p t o", t=PACK),
                in_=weights[x].rearrange("(t p) o -> p t o", t=PACK),
            )

        load_weight(0)
        for x in range(OUTPUTS):
            nc.sync.dma_start(
                out=bias_rows[0:1, x * SIZE : (x + 1) * SIZE],
                in_=biases[x].rearrange("(o n) -> o n", o=1),
            )
        load_attention(0)
        load_values(0)
        load_weight(1)
        load_weight(2)
        for b in range(1, SETS):
            load_values(b)
            load_attention(b)

        attn_grouped, attn_mx = {}, {}
        val_grouped, val_mx = {}, {}
        hidden_grouped, hidden_mx = {}, {}
        w_grouped, w_mx = {}, {}
        flips = {}
        staged = {}

        def regroup(copy, grouped, rows, half):
            runs = SIZE // RUN // 2
            some = slice(half * runs, (half + 1) * runs)
            copy(
                out=grouped[:].rearrange("p (c i t) -> p c t i", i=RUN, t=PACK)[:, some],
                in_=rows[:].rearrange("p (t c i) -> p c t i", t=PACK, i=RUN)[:, some],
            )

        def quantise(name, grouped, bufs):
            columns = grouped.shape[1] // PACK
            words = work.tile([P, columns], U32, name=name + "_words", bufs=bufs, align_bytes=64)
            scales = work.tile([P, columns], U8, name=name + "_scales", bufs=bufs, align_bytes=64)
            nc.vector.quantize_mx(out=words[:].bitcast(FP8X4), scales=scales[:], in_=grouped)
            return words, scales

        def multiply(out, stationary, stationary_cols, moving, moving_cols):
            nc.tensor.matmul_mx(
                out=out,
                lhsT=stationary[0][:, stationary_cols].bitcast(FP8X4),
                lhsT_scale=stationary[1][:, stationary_cols],
                rhs=moving[0][:, moving_cols].bitcast(FP8X4),
                rhs_scale=moving[1][:, moving_cols],
                start=True,
                stop=True,
            )

        def tile_cols(i):
            return slice(i * P, (i + 1) * P)

        def transpose_attention(b):
            words = attn_sb[b][:].bitcast(F32)
            for pair in range(TILES // 2):
                flipped = psum_flip.tile([P, 2, 2, P], F32, name="flipped")
                for i in range(2):
                    for u in range(2):
                        nc.tensor.transpose(
                            flipped[:, i, u, :],
                            words[:, tile_cols(2 * (2 * pair + i) + u)],
                            identity[:],
                        )
                flips[(b, pair)] = flipped

        def group_attention(b, pair):
            if pair == 0:
                attn_grouped[b] = work.tile(
                    [P, PACK * SIZE], BF16, name="attn_grouped", align_bytes=64
                )
            grouped_words = attn_grouped[b][:].bitcast(F32).rearrange(
                "p (j q u) -> p j q u", j=TILES, u=2
            )
            nc.scalar.copy(
                out=grouped_words[:, 2 * pair : 2 * pair + 2, :, :],
                in_=flips[(b, pair)][:].rearrange("p i u q -> p i q u"),
            )

        def quantise_attention(b):
            attn_mx[b] = quantise("attn", attn_grouped[b][:], 3)

        def regroup_values(b, half, copy):
            if half == 0:
                val_grouped[b] = work.tile(
                    [P, PACK * SIZE], BF16, name="val_grouped", align_bytes=64
                )
            regroup(copy, val_grouped[b], val_sb[b], half)

        def quantise_values(b):
            val_mx[b] = quantise("val", val_grouped[b][:], 3)

        def regroup_weight(x, copy):
            w_grouped[x] = work.tile([P, PACK * SIZE], BF16, name="w_grouped", align_bytes=64)
            for half in range(2):
                regroup(copy, w_grouped[x], w_sb[x], half)

        def quantise_weight(x):
            w_mx[x] = quantise("w%d" % x, w_grouped[x][:], 1)

        bias_sb = const.tile([P, OUTPUTS, SIZE], BF16, name="bias_sb")

        def spread_biases():
            for x in range(OUTPUTS):
                spread = psum_out.tile([P, SIZE], BF16, name="spread", tag="projected")
                nc.tensor.matmul(
                    spread[:],
                    lhsT=ones[:],
                    rhs=bias_rows[:, x * SIZE : (x + 1) * SIZE],
                    start=True,
                    stop=True,
                )
                nc.scalar.copy(out=bias_sb[:, x, :], in_=spread[:])

        def hidden_product(b, j, relu=None):
            if j == 0:
                hidden_grouped[b] = work.tile(
                    [P, TILES, P, PACK], BF16, name="hidden_grouped", align_bytes=64
                )
            product = psum_hidden.tile([P, PACK, P], F32, name="product")
            for t in range(PACK):
                multiply(product[:, t, :], val_mx[b], tile_cols(t), attn_mx[b], tile_cols(j))
            hidden = hidden_grouped[b][:, j, :, :]
            read = product[:].rearrange("p t q -> p q t")
            if relu == "vector":
                nc.vector.tensor_scalar_max(hidden, read, 0.0)
            else:
                nc.scalar.activation(out=hidden, in_=read, func=RELU)

        def quantise_hidden(b):
            hidden_mx[b] = quantise(
                "hidden", hidden_grouped[b][:].rearrange("p j q t -> p (j q t)"), 3
            )

        def project_tile(b, x, j):
            if j == 0:
                staged[(b, x)] = staging.tile([P, TILES, SIZE], F32, name="staged")
            rows = staged[(b, x)]
            projected = psum_out.tile([P, SIZE], F32, name="projected")
            multiply(projected[:], hidden_mx[b], tile_cols(j), w_mx[x], slice(0, SIZE))
            if j == GPSIMD_TILE[x]:
                nc.scalar.copy(out=rows[:, j, :], in_=projected[:])
                nc.gpsimd.tensor_tensor(
                    out=rows[:, j, :], in0=rows[:, j, :], in1=bias_sb[:, x, :], op=ADD
                )
            else:
                nc.vector.tensor_tensor(
                    out=rows[:, j, :], in0=projected[:], in1=bias_sb[:, x, :], op=ADD
                )
            last = b == SETS - 1 and x == OUTPUTS - 1
            tiles_per_store = 1 if last else TILES
            if (j + 1) % tiles_per_store == 0:
                done = slice(j + 1 - tiles_per_store, j + 1)
                out_rows = outs[x][b].rearrange("(p j) o -> p j o", j=TILES)
                nc.sync.dma_start(out=out_rows[:, done, :], in_=rows[:, done, :])

        vector_copy, scalar_copy = nc.vector.tensor_copy, nc.scalar.copy
        spread_biases()
        regroup_weight(0, vector_copy)
        quantise_weight(0)
        transpose_attention(0)
        for half in range(2):
            regroup_values(0, half, vector_copy)
        for pair in range(2):
            group_attention(0, pair)
        regroup_weight(1, scalar_copy)
        quantise_values(0)
        quantise_attention(0)
        regroup_weight(2, vector_copy)
        quantise_weight(2)
        quantise_weight(1)
        for j in range(TILES - 1):
            hidden_product(0, j)
        regroup_values(1, 0, vector_copy)
        hidden_product(0, TILES - 1, "vector")
        quantise_hidden(0)
        transpose_attention(1)
        regroup_values(1, 1, vector_copy)
        quantise_values(1)
        for pair in range(2):
            group_attention(1, pair)
        regroup_values(2, 0, scalar_copy)
        quantise_attention(1)

        for b in range(SETS):
            near, far, next_far = b + 1, b + 2, b + 3
            for step in range(OUTPUTS * TILES):
                project_tile(b, step // TILES, step % TILES)
                if far < SETS and step == 1:
                    transpose_attention(far)
                    regroup_values(far, 1, scalar_copy)
                if near < SETS and step in (3, 4, 6, 7):
                    hidden_product(near, (3, 4, 6, 7).index(step))
                if far < SETS and step == 5:
                    quantise_values(far)
                if far < SETS and step in (8, 9):
                    group_attention(far, step - 8)
                if near < SETS and step == 9:
                    quantise_hidden(near)
                if next_far < SETS and step == 9:
                    regroup_values(next_far, 0, scalar_copy)
                if far < SETS and step == 11:
                    quantise_attention(far)
